import numpy as np
import ml_dtypes


def mxq(x, axis, fmt="e4m3"):
    dtype, down = {"e4m3": (ml_dtypes.float8_e4m3fn, 7), "e5m2": (ml_dtypes.float8_e5m2, 14)}[fmt]
    v = np.moveaxis(np.asarray(x, np.float32).astype(ml_dtypes.bfloat16).astype(np.float64), axis, -1)
    blocks = v.reshape(v.shape[:-1] + (-1, 32))
    amax = np.abs(blocks).max(-1, keepdims=True)
    byte = np.maximum(np.where(amax > 0, np.frexp(amax)[1] - 1 + 127, 0) - down, 1)
    scale = np.exp2(byte - 127.0)
    codes = (blocks / scale).astype(np.float32).astype(dtype).astype(np.float64)
    return np.moveaxis((codes * scale).reshape(v.shape), -1, axis)


WIDE = False


def mx_kscale(k):
    if not WIDE:
        return np.ones(k)
    levels = np.array([10, -10, 5, -5, 0])
    if k % 512:
        return np.exp2(np.random.permutation(np.resize(levels, k // 32))).repeat(32)
    a = np.empty((k // 512, 16))
    for p in range(k // 512):
        a[p, :8] = np.random.permutation(np.resize(levels, 8))
        for g in range(8):
            far = levels[np.abs(levels - a[p, g]) >= 10]
            a[p, g + 8] = far[np.random.randint(len(far))]
    return np.exp2(a.ravel()).repeat(32)


BF16 = ml_dtypes.bfloat16


def bf(x):
    return np.asarray(x, np.float32).astype(BF16)


def f64(x):
    return np.asarray(x).astype(np.float64)


B, S, D = 1, 1024, 1024


def sigmoid(z):
    return 1.0 / (1.0 + np.exp(-z))


def draw0():
    s, t = mx_kscale(D), mx_kscale(D)
    return {
        'x': bf(np.random.standard_normal((B, S, D)) * s),
        'wq_w': bf(np.random.standard_normal((D, D)) / np.sqrt(D) / s),
        'wq_b': bf(np.random.standard_normal(D) * 0.1),
        'r_aft': bf(np.random.standard_normal((B, S, D)) * 6.0 / np.sqrt(S) * t),
        'out_w': bf(np.random.standard_normal((D, D)) * 6.0 / np.sqrt(D) / t),
        'out_b': bf(np.random.standard_normal(D) * 0.1),
    }


def core(x, wq_w, wq_b, r_aft, out_w, out_b):
    q = (mxq(f64(x), 2, 'e4m3') @ mxq(f64(wq_w), 1, 'e4m3').T) + f64(wq_b)
    y = sigmoid(q) * f64(r_aft)
    return (mxq(y, 2, 'e4m3') @ mxq(f64(out_w), 1, 'e4m3').T) + f64(out_b)


def e4m3fn_bytes(y):
    return np.clip(np.asarray(y, np.float64), -448.0, 448.0).astype(np.float32).astype(ml_dtypes.float8_e4m3fn).view(np.uint8)


def e4m3fn_values(b):
    return np.asarray(b, np.uint8).view(ml_dtypes.float8_e4m3fn).astype(np.float64)


def setup_inputs():
    d = draw0()
    x0 = np.asarray(d['x']).astype(np.float64)
    s = (np.max(np.abs(x0), axis=(0, 1), keepdims=True) / 448.0).astype(np.float32)
    out = {}
    for k, v in d.items():
        if k == 'x':
            out['x_bytes'] = e4m3fn_bytes(x0 / s.astype(np.float64))
            out['x_scale'] = s
        else:
            out[k] = v
    return out


def reference(x_bytes, x_scale, wq_w, wq_b, r_aft, out_w, out_b):
    return core(e4m3fn_values(x_bytes) * x_scale.astype(np.float64), wq_w, wq_b, r_aft, out_w, out_b)

@@ -1,0 +1,465 @@
+from contextlib import ExitStack
+
+import concourse.mybir as mybir
+from concourse.masks import make_identity
+
+F32 = mybir.dt.float32
+BF16 = mybir.dt.bfloat16
+U32 = mybir.dt.uint32
+U8 = mybir.dt.uint8
+FP8 = mybir.dt.float8_e4m3fn
+FP8X4 = mybir.dt.float8_e4m3fn_x4
+MULT = mybir.AluOpType.mult
+ADD = mybir.AluOpType.add
+SIGMOID = mybir.ActivationFunctionType.Sigmoid
+
+S = 1024
+D = 1024
+FLOPS = 2 * 2 * S * D * D
+P = 128
+NQ = 4
+TQ = S // NQ
+J = TQ // P
+
+
+def tile_aft_full_pb_kernel(tc, x_bytes, x_scale, wq_w, wq_b, r_aft, out_w, out_b, out):
+    nc = tc.nc
+    xb_v = x_bytes[0, :, :].rearrange("(q p j) k -> q p j k", q=NQ, p=P)
+    r_v = r_aft[0, :, :].rearrange("(q p j) k -> q p j k", q=NQ, p=P)
+    out_v = out[0, :, :].rearrange("(q p j) n -> q p j n", q=NQ, p=P)
+    wq_v = wq_w.rearrange("(g m t) k -> g m t k", g=2, m=P)
+    ow_v = out_w.rearrange("(c m s) k -> c m s k", c=2, m=P)
+
+    with ExitStack() as ctx:
+        keep = ctx.enter_context(tc.tile_pool(name="keep", bufs=1))
+        pools = {k: ctx.enter_context(tc.psum_pool(name="p" + k, bufs=b)) for k, b in (('q', 2), ('w', 3), ('x', 3))}
+        ctx.enter_context(tc.manual_schedule())
+
+        sc = keep.tile([P, 2, 4], F32)
+        wqb = keep.tile([P, 2, 4], BF16)
+        outb = keep.tile([P, D], BF16)
+        ident = keep.tile([P, P], F32)
+        warm = keep.tile([P, 1], F32)
+        x_raw = keep.tile([P, NQ, J, D], U8, align_bytes=64)
+        x_bf = keep.tile([P, NQ, J, D], BF16, align_bytes=64)
+        wq_raw = keep.tile([P, 8, D], BF16, align_bytes=64)
+        ow_raw = keep.tile([P, 2, 4, D], BF16, align_bytes=64)
+        r_raw = keep.tile([P, NQ, J, D], BF16, align_bytes=64)
+        xg = keep.tile([P, NQ, 2, TQ * 4], BF16, align_bytes=64)
+        x_codes = keep.tile([P, NQ, 2, TQ], U32, align_bytes=64)
+        x_scales = keep.tile([P, NQ, 2, TQ], U8, align_bytes=64)
+        wg = keep.tile([P, 8, 2, P * 4], BF16, align_bytes=64)
+        w_codes = keep.tile([P, 8, 2, P], U32, align_bytes=64)
+        w_scales = keep.tile([P, 8, 2, P], U8, align_bytes=64)
+        og = keep.tile([P, 2, 2, 4, P * 4], BF16, align_bytes=64)
+        o_codes = keep.tile([P, 2, 2, 512], U32, align_bytes=64)
+        o_scales = keep.tile([P, 2, 2, 512], U8, align_bytes=64)
+        sg = keep.tile([P, 2, 2, 4, TQ], F32, align_bytes=64)
+        yg = keep.tile([P, NQ, 2, TQ * 4], BF16, align_bytes=64)
+        y_codes = keep.tile([P, NQ, 2, TQ], U32, align_bytes=64)
+        y_scales = keep.tile([P, NQ, 2, TQ], U8, align_bytes=64)
+        res = keep.tile([P, NQ, J, D], F32, align_bytes=64)
+        bank = {}
+
+        x_words = x_bf[:].bitcast(F32)
+        r_words = r_raw[:].bitcast(F32)
+        w_words = wq_raw[:].bitcast(F32)
+        o_words = ow_raw[:].bitcast(F32)
+        wg_words = wg[:].bitcast(F32)
+        og_words = og[:].bitcast(F32)
+
+        def sc_():
+            nc.scalar.dma_start(out=sc[:], in_=x_scale[0, :, :].rearrange("o (g p t) -> p (o g) t", p=P, t=4))
+
+        def bq():
+            nc.scalar.dma_start(out=wqb[:], in_=wq_b.rearrange("(g p t) -> p g t", p=P, t=4))
+
+        def id_():
+            make_identity(nc, ident[:])
+            nc.vector.memset(warm[:], 0.0)
+            nc.scalar.activation(out=warm[:], in_=warm[:], func=SIGMOID)
+
+        def lx(q):
+            nc.sync.dma_start(out=x_raw[:, q], in_=xb_v[q])
+
+        def l1(s):
+            nc.sync.dma_start(out=wq_raw[:, s, :], in_=wq_v[s // 4][:, s % 4, :])
+
+        def lw(i):
+            g, t = i // 2, 2 * (i % 2)
+            nc.sync.dma_start(out=wq_raw[:, 2 * i : 2 * i + 2, :], in_=wq_v[g][:, t : t + 2, :])
+
+        def lo(i):
+            c, s = i // 2, 2 * (i % 2)
+            nc.sync.dma_start(out=ow_raw[:, c, s : s + 2, :], in_=ow_v[c][:, s : s + 2, :])
+
+        def lr(q):
+            nc.sync.dma_start(out=r_raw[:, q], in_=r_v[q])
+
+        def lb():
+            nc.sync.dma_start(out=outb[:], in_=out_b.partition_broadcast(P))
+
+        def cast(q, j, e):
+            src = x_raw[:, q, j, :].bitcast(FP8)
+            if e == "V":
+                nc.vector.tensor_copy(out=x_bf[:, q, j, :], in_=src)
+            else:
+                nc.scalar.copy(out=x_bf[:, q, j, :], in_=src)
+
+        def copy(e, dst, src):
+            if e == "V":
+                nc.vector.tensor_copy(out=dst, in_=src)
+            else:
+                nc.scalar.copy(out=dst, in_=src)
+
+        def turn_tokens(words, q, g):
+            b = pools["x"].tile([P, 2, TQ], F32, name="x")
+            for u in range(2):
+                for j in range(J):
+                    nc.tensor.transpose(
+                        b[:, u, j * P : (j + 1) * P],
+                        words[:, q, j, 256 * g + u : 256 * (g + 1) : 2],
+                        ident[:],
+                    )
+            return b
+
+        def turn_rows(row_words):
+            b = pools["w"].tile([P, 4, P], F32, name="w")
+            for i in range(4):
+                g, u = i // 2, i % 2
+                nc.tensor.transpose(b[:, i, :], row_words[:, 256 * g + u : 256 * (g + 1) : 2], ident[:])
+            return b
+
+        def by_k(flat):
+            return flat.rearrange("p (c u e) -> p c u e", u=2, e=2)
+
+        def bank_by_k(b):
+            return b[:].bitcast(BF16).rearrange("p u (c e) -> p c u e", e=2)
+
+        def xT(q, g):
+            bank["x", q, g] = turn_tokens(x_words, q, g)
+
+        def xS(q, g):
+            scale = sc[:, g, :].rearrange("p (u e) -> p u e", u=2).unsqueeze(1).to_broadcast([P, TQ, 2, 2])
+            nc.vector.tensor_tensor(out=by_k(xg[:, q, g, :]), in0=bank_by_k(bank["x", q, g]), in1=scale, op=MULT)
+
+        def xq(q):
+            nc.vector.quantize_mx(
+                out=x_codes[:, q].rearrange("p g c -> p (g c)").bitcast(FP8X4),
+                scales=x_scales[:, q].rearrange("p g c -> p (g c)"),
+                in_=xg[:, q].rearrange("p g c -> p (g c)"),
+            )
+
+        def wT(i):
+            bank["w", i] = turn_rows(w_words[:, i, :])
+
+        def wC(i, e):
+            copy(
+                e,
+                wg_words[:, i].rearrange("p g (m u) -> p g m u", u=2),
+                bank["w", i][:].rearrange("p (g u) m -> p g m u", u=2),
+            )
+
+        def wq(i):
+            pair = slice(2 * i, 2 * i + 2)
+            nc.vector.quantize_mx(
+                out=w_codes[:, pair].rearrange("p s g m -> p (s g m)").bitcast(FP8X4),
+                scales=w_scales[:, pair].rearrange("p s g m -> p (s g m)"),
+                in_=wg[:, pair].rearrange("p s g m -> p (s g m)"),
+            )
+
+        def oT(c, s):
+            bank["o", c, s] = turn_rows(o_words[:, c, s, :])
+
+        def oC(c, s, e):
+            copy(
+                e,
+                og_words[:, c, :, s, :].rearrange("p g (m u) -> p g m u", u=2),
+                bank["o", c, s][:].rearrange("p (g u) m -> p g m u", u=2),
+            )
+
+        def oq(c, g):
+            nc.vector.quantize_mx(
+                out=o_codes[:, c, g, :].bitcast(FP8X4),
+                scales=o_scales[:, c, g, :],
+                in_=og[:, c, g].rearrange("p s m -> p (s m)"),
+            )
+
+        def rT(q, f):
+            bank["r", q, f] = turn_tokens(r_words, q, f)
+
+        def mm(q, f, h):
+            b = pools["q"].tile([P, 2, TQ], F32, name="q")
+            bank["q", q, f, h] = b
+            for i in range(2):
+                t = 2 * h + i
+                for g in range(2):
+                    nc.tensor.matmul_mx(
+                        out=b[:, i, :],
+                        lhsT=w_codes[:, 4 * f + t, g, :].bitcast(FP8X4),
+                        lhsT_scale=w_scales[:, 4 * f + t, g, :],
+                        rhs=x_codes[:, q, g, :].bitcast(FP8X4),
+                        rhs_scale=x_scales[:, q, g, :],
+                        start=(g == 0),
+                        stop=(g == 1),
+                    )
+
+        def sig(q, f, h):
+            for i in range(2):
+                t = 2 * h + i
+                nc.scalar.activation(
+                    out=sg[:, q % 2, f, t, :], in_=bank["q", q, f, h][:, i, :], func=SIGMOID, bias=wqb[:, f, t : t + 1]
+                )
+
+        def gate(q, f):
+            nc.vector.tensor_tensor(
+                out=by_k(yg[:, q, f, :]),
+                in0=bank_by_k(bank["r", q, f]),
+                in1=sg[:, q % 2, f].rearrange("p (u e) c -> p c u e", u=2),
+                op=MULT,
+            )
+
+        def yq(q):
+            nc.vector.quantize_mx(
+                out=y_codes[:, q].rearrange("p g c -> p (g c)").bitcast(FP8X4),
+                scales=y_scales[:, q].rearrange("p g c -> p (g c)"),
+                in_=yg[:, q].rearrange("p g c -> p (g c)"),
+            )
+
+        def yq1(q, f):
+            nc.vector.quantize_mx(
+                out=y_codes[:, q, f, :].bitcast(FP8X4),
+                scales=y_scales[:, q, f, :],
+                in_=yg[:, q, f, :],
+            )
+
+        def out_(q, j, c):
+            b = pools["w"].tile([P, 512], F32, name="w")
+            bank["out", q, j, c] = b
+            for g in range(2):
+                nc.tensor.matmul_mx(
+                    out=b[:],
+                    lhsT=y_codes[:, q, g, j * P : (j + 1) * P].bitcast(FP8X4),
+                    lhsT_scale=y_scales[:, q, g, j * P : (j + 1) * P],
+                    rhs=o_codes[:, c, g, :].bitcast(FP8X4),
+                    rhs_scale=o_scales[:, c, g, :],
+                    start=(g == 0),
+                    stop=(g == 1),
+                )
+
+        def bias(q, j, c):
+            cols = slice(512 * c, 512 * (c + 1))
+            nc.vector.tensor_tensor(
+                out=res[:, q, j, cols].rearrange("p (m s) -> p m s", s=4),
+                in0=bank["out", q, j, c][:].rearrange("p (s m) -> p m s", s=4),
+                in1=outb[:, cols].rearrange("p (m s) -> p m s", s=4),
+                op=ADD,
+            )
+
+        def biasC(q, j, c):
+            cols = slice(512 * c, 512 * (c + 1))
+            nc.scalar.copy(
+                out=res[:, q, j, cols].rearrange("p (m s) -> p m s", s=4),
+                in_=bank["out", q, j, c][:].rearrange("p (s m) -> p m s", s=4),
+            )
+
+        def biasP(q, j, c):
+            cols = slice(512 * c, 512 * (c + 1))
+            nc.gpsimd.tensor_tensor(out=res[:, q, j, cols], in0=res[:, q, j, cols], in1=outb[:, cols], op=ADD)
+
+        def st(q, j):
+            nc.sync.dma_start(out=out_v[q][:, j, :], in_=res[:, q, j, :])
+
+        def st1(q, j, c):
+            cols = slice(512 * c, 512 * (c + 1))
+            nc.sync.dma_start(out=out_v[q][:, j, cols], in_=res[:, q, j, cols])
+
+        bq()
+        id_()
+        lx(0)
+        sc_()
+        lx(1)
+        lw(1)
+        lw(2)
+        l1(1)
+        lw(3)
+        l1(0)
+        lo(1)
+        lx(2)
+        cast(0, 0, "V")
+        cast(0, 1, "S")
+        lo(0)
+        cast(1, 0, "S")
+        xT(0, 1)
+        lr(2)
+        wT(2)
+        xS(0, 1)
+        xT(0, 0)
+        cast(1, 1, "S")
+        lo(3)
+        wT(3)
+        xS(0, 0)
+        lo(2)
+        wT(5)
+        wC(2, "S")
+        xT(1, 0)
+        wC(3, "S")
+        xT(1, 1)
+        lr(0)
+        xS(1, 0)
+        wT(7)
+        wC(5, "S")
+        lx(3)
+        wT(0)
+        wC(7, "S")
+        wq(1)
+        wT(1)
+        lr(1)
+        wC(0, "S")
+        xq(0)
+        wT(4)
+        lb()
+        wC(1, "S")
+        wT(6)
+        xS(1, 1)
+        wC(4, "S")
+        oT(0, 2)
+        lr(3)
+        cast(2, 0, "S")
+        mm(0, 0, 1)
+        wq(0)
+        oC(0, 2, "V")
+        mm(0, 0, 0)
+        wC(6, "S")
+        wq(2)
+        oT(0, 0)
+        cast(2, 1, "S")
+        oT(0, 3)
+        wq(3)
+        oT(0, 1)
+        oC(0, 0, "V")
+        sig(0, 0, 1)
+        xT(2, 1)
+        xq(1)
+        xT(2, 0)
+        sig(0, 0, 0)
+        xS(2, 1)
+        mm(0, 1, 0)
+        oC(0, 3, "S")
+        mm(0, 1, 1)
+        sig(0, 1, 0)
+        xS(2, 0)
+        oT(1, 3)
+        rT(0, 0)
+        sig(0, 1, 1)
+        rT(0, 1)
+        gate(0, 0)
+        oC(0, 1, "S")
+        rT(1, 1)
+        oC(1, 3, "S")
+        oT(1, 0)
+        oq(0, 0)
+        mm(1, 0, 1)
+        cast(3, 0, "S")
+        mm(1, 1, 1)
+        xq(2)
+        oT(1, 1)
+        gate(0, 1)
+        sig(1, 0, 1)
+        sig(1, 1, 1)
+        mm(1, 1, 0)
+        oC(1, 1, "V")
+        mm(1, 0, 0)
+        sig(1, 1, 0)
+        yq(0)
+        rT(1, 0)
+        sig(1, 0, 0)
+        oq(0, 1)
+        mm(2, 1, 0)
+        cast(3, 1, "S")
+        gate(1, 1)
+        out_(0, 1, 0)
+        mm(2, 1, 1)
+        oC(1, 0, "S")
+        bias(0, 1, 0)
+        xT(3, 0)
+        sig(2, 1, 1)
+        xT(3, 1)
+        gate(1, 0)
+        oT(1, 2)
+        sig(2, 1, 0)
+        out_(0, 0, 0)
+        xS(3, 0)
+        oC(1, 2, "S")
+        mm(2, 0, 1)
+        rT(2, 0)
+        xS(3, 1)
+        rT(3, 0)
+        yq(1)
+        rT(2, 1)
+        mm(2, 0, 0)
+        oq(1, 1)
+        out_(1, 0, 0)
+        oq(1, 0)
+        sig(2, 0, 0)
+        bias(0, 0, 0)
+        sig(2, 0, 1)
+        out_(0, 0, 1)
+        xq(3)
+        out_(0, 1, 1)
+        biasC(0, 0, 1)
+        bias(1, 0, 0)
+        mm(3, 0, 1)
+        biasC(0, 1, 1)
+        biasP(0, 0, 1)
+        gate(2, 1)
+        mm(3, 0, 0)
+        sig(3, 0, 1)
+        out_(1, 1, 1)
+        biasP(0, 1, 1)
+        st(0, 0)
+        gate(2, 0)
+        out_(1, 0, 1)
+        biasC(1, 1, 1)
+        out_(1, 1, 0)
+        sig(3, 0, 0)
+        biasP(1, 1, 1)
+        mm(3, 1, 0)
+        st(0, 1)
+        yq(2)
+        biasC(1, 0, 1)
+        mm(3, 1, 1)
+        bias(1, 1, 0)
+        sig(3, 1, 0)
+        out_(2, 1, 1)
+        biasP(1, 0, 1)
+        gate(3, 0)
+        out_(2, 1, 0)
+        st(1, 1)
+        sig(3, 1, 1)
+        rT(3, 1)
+        biasC(2, 1, 1)
+        st(1, 0)
+        bias(2, 1, 0)
+        out_(2, 0, 1)
+        biasP(2, 1, 1)
+        out_(2, 0, 0)
+        gate(3, 1)
+        biasC(2, 0, 1)
+        biasP(2, 0, 1)
+        st(2, 1)
+        yq(3)
+        bias(2, 0, 0)
+        out_(3, 1, 0)
+        out_(3, 0, 0)
+        st(2, 0)
+        bias(3, 1, 0)
+        out_(3, 1, 1)
+        bias(3, 0, 0)
+        st1(3, 1, 0)
+        out_(3, 0, 1)
+        bias(3, 1, 1)
+        st1(3, 0, 0)
+        bias(3, 0, 1)
+        st1(3, 1, 1)
+        st1(3, 0, 1)

@@ -40,6 +40,7 @@ def tile_aft_full_pb_kernel(tc, x_bytes, x_scale, wq_w, wq_b, r_aft, out_w, out_
         outb = keep.tile([P, D], BF16)
         ident = keep.tile([P, P], F32)
         warm = keep.tile([P, 1], F32)
+        zz = keep.tile([P, 512], BF16)
         x_raw = keep.tile([P, NQ, J, D], U8, align_bytes=64)
         x_bf = keep.tile([P, NQ, J, D], BF16, align_bytes=64)
         wq_raw = keep.tile([P, 8, D], BF16, align_bytes=64)
@@ -76,6 +77,7 @@ def tile_aft_full_pb_kernel(tc, x_bytes, x_scale, wq_w, wq_b, r_aft, out_w, out_
 
         def id_():
             make_identity(nc, ident[:])
+            nc.vector.memset(zz[:], 0.0)
             nc.vector.memset(warm[:], 0.0)
             nc.scalar.activation(out=warm[:], in_=warm[:], func=SIGMOID)
 
@@ -112,8 +114,13 @@ def tile_aft_full_pb_kernel(tc, x_bytes, x_scale, wq_w, wq_b, r_aft, out_w, out_
             else:
                 nc.scalar.copy(out=dst, in_=src)
 
-        def turn_tokens(words, q, g):
+        def busy(flat, n):
+            for i in range(n):
+                nc.tensor.matmul(flat, lhsT=zz[:, :P], rhs=zz[:], start=True, stop=True)
+
+        def turn_tokens(words, q, g, n):
             b = pools["x"].tile([P, 2, TQ], F32, name="x")
+            busy(b[:].rearrange("p u c -> p (u c)"), n)
             for u in range(2):
                 for j in range(J):
                     nc.tensor.transpose(
@@ -123,8 +130,9 @@ def tile_aft_full_pb_kernel(tc, x_bytes, x_scale, wq_w, wq_b, r_aft, out_w, out_
                     )
             return b
 
-        def turn_rows(row_words):
+        def turn_rows(row_words, n):
             b = pools["w"].tile([P, 4, P], F32, name="w")
+            busy(b[:].rearrange("p i m -> p (i m)"), n)
             for i in range(4):
                 g, u = i // 2, i % 2
                 nc.tensor.transpose(b[:, i, :], row_words[:, 256 * g + u : 256 * (g + 1) : 2], ident[:])
@@ -136,8 +144,8 @@ def tile_aft_full_pb_kernel(tc, x_bytes, x_scale, wq_w, wq_b, r_aft, out_w, out_
         def bank_by_k(b):
             return b[:].bitcast(BF16).rearrange("p u (c e) -> p c u e", e=2)
 
-        def xT(q, g):
-            bank["x", q, g] = turn_tokens(x_words, q, g)
+        def xT(q, g, n=0):
+            bank["x", q, g] = turn_tokens(x_words, q, g, n)
 
         def xS(q, g):
             scale = sc[:, g, :].rearrange("p (u e) -> p u e", u=2).unsqueeze(1).to_broadcast([P, TQ, 2, 2])
@@ -150,8 +158,8 @@ def tile_aft_full_pb_kernel(tc, x_bytes, x_scale, wq_w, wq_b, r_aft, out_w, out_
                 in_=xg[:, q].rearrange("p g c -> p (g c)"),
             )
 
-        def wT(i):
-            bank["w", i] = turn_rows(w_words[:, i, :])
+        def wT(i, n=0):
+            bank["w", i] = turn_rows(w_words[:, i, :], n)
 
         def wC(i, e):
             copy(
@@ -168,8 +176,8 @@ def tile_aft_full_pb_kernel(tc, x_bytes, x_scale, wq_w, wq_b, r_aft, out_w, out_
                 in_=wg[:, pair].rearrange("p s g m -> p (s g m)"),
             )
 
-        def oT(c, s):
-            bank["o", c, s] = turn_rows(o_words[:, c, s, :])
+        def oT(c, s, n=0):
+            bank["o", c, s] = turn_rows(o_words[:, c, s, :], n)
 
         def oC(c, s, e):
             copy(
@@ -185,12 +193,13 @@ def tile_aft_full_pb_kernel(tc, x_bytes, x_scale, wq_w, wq_b, r_aft, out_w, out_
                 in_=og[:, c, g].rearrange("p s m -> p (s m)"),
             )
 
-        def rT(q, f):
-            bank["r", q, f] = turn_tokens(r_words, q, f)
+        def rT(q, f, n=0):
+            bank["r", q, f] = turn_tokens(r_words, q, f, n)
 
-        def mm(q, f, h):
+        def mm(q, f, h, n=0):
             b = pools["q"].tile([P, 2, TQ], F32, name="q")
             bank["q", q, f, h] = b
+            busy(b[:].rearrange("p u c -> p (u c)"), n)
             for i in range(2):
                 t = 2 * h + i
                 for g in range(2):
@@ -233,9 +242,10 @@ def tile_aft_full_pb_kernel(tc, x_bytes, x_scale, wq_w, wq_b, r_aft, out_w, out_
                 in_=yg[:, q, f, :],
             )
 
-        def out_(q, j, c):
+        def out_(q, j, c, n=0):
             b = pools["w"].tile([P, 512], F32, name="w")
             bank["out", q, j, c] = b
+            busy(b[:], n)
             for g in range(2):
                 nc.tensor.matmul_mx(
                     out=b[:],
@@ -274,192 +284,192 @@ def tile_aft_full_pb_kernel(tc, x_bytes, x_scale, wq_w, wq_b, r_aft, out_w, out_
             cols = slice(512 * c, 512 * (c + 1))
             nc.sync.dma_start(out=out_v[q][:, j, cols], in_=res[:, q, j, cols])
 
-        bq()
-        id_()
-        lx(0)
         sc_()
-        lx(1)
-        lw(1)
+        id_()
         lw(2)
-        l1(1)
-        lw(3)
-        l1(0)
-        lo(1)
-        lx(2)
-        cast(0, 0, "V")
-        cast(0, 1, "S")
-        lo(0)
-        cast(1, 0, "S")
-        xT(0, 1)
-        lr(2)
-        wT(2)
-        xS(0, 1)
-        xT(0, 0)
-        cast(1, 1, "S")
-        lo(3)
-        wT(3)
-        xS(0, 0)
-        lo(2)
-        wT(5)
-        wC(2, "S")
-        xT(1, 0)
-        wC(3, "S")
-        xT(1, 1)
-        lr(0)
-        xS(1, 0)
-        wT(7)
-        wC(5, "S")
+        lx(0)
+        lx(1)
         lx(3)
-        wT(0)
-        wC(7, "S")
-        wq(1)
-        wT(1)
+        lw(1)
+        l1(0)
+        lx(2)
+        lw(3)
+        l1(1)
+        wT(4, n=5)
         lr(1)
-        wC(0, "S")
-        xq(0)
-        wT(4)
-        lb()
-        wC(1, "S")
-        wT(6)
-        xS(1, 1)
+        cast(0, 1, "V")
+        wT(5, n=1)
+        lo(2)
+        cast(1, 0, "S")
+        cast(0, 0, "V")
+        lo(1)
+        cast(1, 1, "V")
+        xT(0, 0)
+        bq()
+        cast(3, 1, "V")
         wC(4, "S")
-        oT(0, 2)
-        lr(3)
-        cast(2, 0, "S")
-        mm(0, 0, 1)
-        wq(0)
-        oC(0, 2, "V")
-        mm(0, 0, 0)
-        wC(6, "S")
-        wq(2)
-        oT(0, 0)
-        cast(2, 1, "S")
-        oT(0, 3)
-        wq(3)
-        oT(0, 1)
-        oC(0, 0, "V")
-        sig(0, 0, 1)
-        xT(2, 1)
-        xq(1)
-        xT(2, 0)
-        sig(0, 0, 0)
-        xS(2, 1)
-        mm(0, 1, 0)
-        oC(0, 3, "S")
-        mm(0, 1, 1)
-        sig(0, 1, 0)
-        xS(2, 0)
-        oT(1, 3)
-        rT(0, 0)
-        sig(0, 1, 1)
-        rT(0, 1)
-        gate(0, 0)
-        oC(0, 1, "S")
-        rT(1, 1)
-        oC(1, 3, "S")
-        oT(1, 0)
-        oq(0, 0)
-        mm(1, 0, 1)
+        lo(0)
+        xT(1, 1, n=1)
+        xS(0, 0)
         cast(3, 0, "S")
-        mm(1, 1, 1)
-        xq(2)
-        oT(1, 1)
-        gate(0, 1)
-        sig(1, 0, 1)
-        sig(1, 1, 1)
-        mm(1, 1, 0)
-        oC(1, 1, "V")
-        mm(1, 0, 0)
-        sig(1, 1, 0)
-        yq(0)
-        rT(1, 0)
-        sig(1, 0, 0)
-        oq(0, 1)
-        mm(2, 1, 0)
-        cast(3, 1, "S")
-        gate(1, 1)
-        out_(0, 1, 0)
-        mm(2, 1, 1)
-        oC(1, 0, "S")
-        bias(0, 1, 0)
-        xT(3, 0)
-        sig(2, 1, 1)
-        xT(3, 1)
-        gate(1, 0)
-        oT(1, 2)
-        sig(2, 1, 0)
-        out_(0, 0, 0)
-        xS(3, 0)
-        oC(1, 2, "S")
-        mm(2, 0, 1)
-        rT(2, 0)
+        lo(3)
+        xT(0, 1)
+        lb()
+        wT(0)
+        xS(1, 1)
+        wT(3)
+        wC(0, "S")
+        lr(0)
+        xS(0, 1)
+        wC(5, "S")
+        xT(3, 1, n=1)
+        lr(2)
+        wC(3, "S")
+        wT(1)
+        cast(2, 0, "V")
+        wT(2)
+        wC(1, "S")
+        xq(0)
+        lr(3)
+        xT(1, 0)
+        wC(2, "S")
+        wq(2)
+        xT(3, 0, n=1)
+        wq(0)
+        wT(7)
+        xS(1, 0)
+        oT(1, 0)
+        wC(7, "S")
+        mm(0, 0, 0)
         xS(3, 1)
-        rT(3, 0)
-        yq(1)
-        rT(2, 1)
-        mm(2, 0, 0)
-        oq(1, 1)
-        out_(1, 0, 0)
-        oq(1, 0)
-        sig(2, 0, 0)
-        bias(0, 0, 0)
-        sig(2, 0, 1)
-        out_(0, 0, 1)
+        oC(1, 0, "S")
+        oT(0, 2)
+        cast(2, 1, "S")
+        xq(1)
+        wT(6)
+        wq(1)
+        mm(0, 1, 0)
+        oC(0, 2, "S")
+        xS(3, 0)
+        sig(0, 0, 0)
+        xT(2, 0)
+        sig(0, 1, 0)
+        oT(1, 1)
+        mm(1, 1, 0)
+        wC(6, "S")
+        oT(0, 0)
+        wq(3)
+        sig(1, 1, 0)
+        xT(2, 1)
+        xS(2, 0)
+        oC(1, 1, "S")
+        oT(0, 3)
+        rT(0, 1)
+        oC(0, 3, "S")
+        xS(2, 1)
+        mm(1, 1, 1)
+        mm(0, 1, 1)
         xq(3)
+        sig(1, 1, 1)
+        oT(1, 3)
+        sig(0, 1, 1)
+        rT(0, 0)
+        oC(0, 0, "S")
+        gate(0, 1)
+        mm(0, 0, 1)
+        oC(1, 3, "S")
+        mm(1, 0, 0)
+        sig(0, 0, 1)
+        xq(2)
+        oT(1, 2)
+        sig(1, 0, 0)
+        gate(0, 0)
+        rT(1, 0)
+        oC(1, 2, "S")
+        rT(1, 1)
+        oq(1, 1)
+        mm(1, 0, 1)
+        yq(0)
+        oT(0, 1)
+        sig(1, 0, 1)
+        oq(1, 0)
+        rT(2, 0)
+        gate(1, 0)
+        mm(2, 0, 1)
+        out_(0, 0, 1)
+        sig(2, 0, 1)
+        gate(1, 1)
         out_(0, 1, 1)
-        biasC(0, 0, 1)
-        bias(1, 0, 0)
+        oC(0, 1, "S")
+        mm(2, 1, 1)
+        oq(0, 1)
+        rT(2, 1)
+        sig(2, 1, 1)
+        oq(0, 0)
         mm(3, 0, 1)
-        biasC(0, 1, 1)
-        biasP(0, 0, 1)
-        gate(2, 1)
-        mm(3, 0, 0)
+        yq(1)
+        mm(2, 1, 0)
         sig(3, 0, 1)
+        bias(0, 0, 1)
+        out_(0, 0, 0)
+        sig(2, 1, 0)
+        mm(2, 0, 0)
+        biasC(0, 1, 1)
+        gate(2, 1)
         out_(1, 1, 1)
+        sig(2, 0, 0)
         biasP(0, 1, 1)
-        st(0, 0)
+        mm(3, 0, 0)
+        biasC(0, 0, 0)
         gate(2, 0)
-        out_(1, 0, 1)
-        biasC(1, 1, 1)
         out_(1, 1, 0)
         sig(3, 0, 0)
-        biasP(1, 1, 1)
         mm(3, 1, 0)
-        st(0, 1)
-        yq(2)
-        biasC(1, 0, 1)
-        mm(3, 1, 1)
-        bias(1, 1, 0)
+        biasP(0, 0, 0)
+        biasC(1, 1, 0)
+        rT(3, 0)
+        bias(1, 1, 1)
         sig(3, 1, 0)
-        out_(2, 1, 1)
-        biasP(1, 0, 1)
+        yq(2)
+        out_(0, 1, 0)
+        st(0, 0)
         gate(3, 0)
-        out_(2, 1, 0)
-        st(1, 1)
-        sig(3, 1, 1)
-        rT(3, 1)
-        biasC(2, 1, 1)
-        st(1, 0)
-        bias(2, 1, 0)
-        out_(2, 0, 1)
-        biasP(2, 1, 1)
+        biasP(1, 1, 0)
+        mm(3, 1, 1)
         out_(2, 0, 0)
+        sig(3, 1, 1)
+        bias(0, 1, 0)
+        out_(2, 0, 1)
+        st(1, 1)
+        biasC(2, 0, 0)
+        yq1(3, 0)
+        rT(3, 1)
+        st(0, 1)
+        bias(2, 0, 1)
+        biasP(2, 0, 0)
+        out_(2, 1, 0)
         gate(3, 1)
-        biasC(2, 0, 1)
-        biasP(2, 0, 1)
-        st(2, 1)
-        yq(3)
-        bias(2, 0, 0)
-        out_(3, 1, 0)
-        out_(3, 0, 0)
+        out_(1, 0, 1)
+        biasC(2, 1, 0)
         st(2, 0)
-        bias(3, 1, 0)
+        out_(1, 0, 0)
+        bias(1, 0, 1)
+        biasP(2, 1, 0)
+        out_(2, 1, 1)
+        bias(1, 0, 0)
+        st(1, 0)
+        yq1(3, 1)
+        bias(2, 1, 1)
+        out_(3, 0, 1)
+        out_(3, 0, 0)
+        st(2, 1)
+        bias(3, 0, 1)
         out_(3, 1, 1)
         bias(3, 0, 0)
-        st1(3, 1, 0)
-        out_(3, 0, 1)
+        st1(3, 0, 1)
+        out_(3, 1, 0)
         bias(3, 1, 1)
         st1(3, 0, 0)
-        bias(3, 0, 1)
+        bias(3, 1, 0)
         st1(3, 1, 1)
-        st1(3, 0, 1)
+        st1(3, 1, 0)

@@ -28,7 +28,7 @@ def tile_aft_full_pb_kernel(tc, x_bytes, x_scale, wq_w, wq_b, r_aft, out_w, out_
     r_v = r_aft[0, :, :].rearrange("(q p j) k -> q p j k", q=NQ, p=P)
     out_v = out[0, :, :].rearrange("(q p j) n -> q p j n", q=NQ, p=P)
     wq_v = wq_w.rearrange("(g m t) k -> g m t k", g=2, m=P)
-    ow_v = out_w.rearrange("(c m s) k -> c m s k", c=2, m=P)
+    ow_v = out_w.rearrange("(c s m) k -> c m s k", c=2, m=P)
 
     with ExitStack() as ctx:
         keep = ctx.enter_context(tc.tile_pool(name="keep", bufs=1))
@@ -260,18 +260,12 @@ def tile_aft_full_pb_kernel(tc, x_bytes, x_scale, wq_w, wq_b, r_aft, out_w, out_
         def bias(q, j, c):
             cols = slice(512 * c, 512 * (c + 1))
             nc.vector.tensor_tensor(
-                out=res[:, q, j, cols].rearrange("p (m s) -> p m s", s=4),
-                in0=bank["out", q, j, c][:].rearrange("p (s m) -> p m s", s=4),
-                in1=outb[:, cols].rearrange("p (m s) -> p m s", s=4),
-                op=ADD,
+                out=res[:, q, j, cols], in0=bank["out", q, j, c][:], in1=outb[:, cols], op=ADD
             )
 
         def biasC(q, j, c):
             cols = slice(512 * c, 512 * (c + 1))
-            nc.scalar.copy(
-                out=res[:, q, j, cols].rearrange("p (m s) -> p m s", s=4),
-                in_=bank["out", q, j, c][:].rearrange("p (s m) -> p m s", s=4),
-            )
+            nc.scalar.copy(out=res[:, q, j, cols], in_=bank["out", q, j, c][:])
 
         def biasP(q, j, c):
             cols = slice(512 * c, 512 * (c + 1))
@@ -284,192 +278,193 @@ def tile_aft_full_pb_kernel(tc, x_bytes, x_scale, wq_w, wq_b, r_aft, out_w, out_
             cols = slice(512 * c, 512 * (c + 1))
             nc.sync.dma_start(out=out_v[q][:, j, cols], in_=res[:, q, j, cols])
 
-        sc_()
-        id_()
-        lw(2)
-        lx(0)
-        lx(1)
-        lx(3)
-        lw(1)
-        l1(0)
-        lx(2)
-        lw(3)
-        l1(1)
-        wT(4, n=5)
-        lr(1)
-        cast(0, 1, "V")
-        wT(5, n=1)
-        lo(2)
-        cast(1, 0, "S")
-        cast(0, 0, "V")
-        lo(1)
-        cast(1, 1, "V")
-        xT(0, 0)
         bq()
-        cast(3, 1, "V")
-        wC(4, "S")
+        id_()
+        lx(0)
+        sc_()
+        lw(2)
+        lw(1)
+        l1(1)
+        lw(3)
+        l1(0)
+        lx(1)
+        lx(2)
         lo(0)
-        xT(1, 1, n=1)
-        xS(0, 0)
-        cast(3, 0, "S")
-        lo(3)
-        xT(0, 1)
-        lb()
-        wT(0)
-        xS(1, 1)
-        wT(3)
-        wC(0, "S")
-        lr(0)
-        xS(0, 1)
-        wC(5, "S")
-        xT(3, 1, n=1)
-        lr(2)
-        wC(3, "S")
-        wT(1)
-        cast(2, 0, "V")
-        wT(2)
-        wC(1, "S")
-        xq(0)
+        cast(0, 1, "S")
+        lx(3)
+        cast(0, 0, "S")
+        wT(5, n=8)
+        wT(4)
+        wC(5, "V")
         lr(3)
-        xT(1, 0)
-        wC(2, "S")
+        xT(0, 1)
+        wC(4, "S")
+        lr(0)
+        wT(3)
+        xS(0, 1)
+        wT(2)
+        lr(2)
         wq(2)
-        xT(3, 0, n=1)
-        wq(0)
+        xT(0, 0)
+        wC(2, "S")
+        lo(3)
+        wC(3, "V")
         wT(7)
-        xS(1, 0)
-        oT(1, 0)
-        wC(7, "S")
-        mm(0, 0, 0)
-        xS(3, 1)
-        oC(1, 0, "S")
-        oT(0, 2)
-        cast(2, 1, "S")
-        xq(1)
+        lr(1)
+        xS(0, 0)
         wT(6)
+        lo(2)
+        wC(7, "S")
+        wT(0)
+        cast(1, 1, "S")
         wq(1)
-        mm(0, 1, 0)
-        oC(0, 2, "S")
-        xS(3, 0)
-        sig(0, 0, 0)
-        xT(2, 0)
-        sig(0, 1, 0)
-        oT(1, 1)
-        mm(1, 1, 0)
+        lo(1)
+        wT(1)
+        xq(0)
         wC(6, "S")
-        oT(0, 0)
+        lb()
+        wC(1, "V")
+        mm(0, 0, 1)
+        cast(1, 0, "S")
         wq(3)
+        mm(0, 1, 0)
+        cast(3, 0, "V")
+        wC(0, "S")
+        xT(1, 0)
+        sig(0, 0, 1)
+        wq(0)
+        xT(1, 1)
+        sig(0, 1, 0)
+        xS(1, 0)
+        oT(0, 1)
+        cast(3, 1, "S")
+        mm(0, 0, 0)
+        xS(1, 1)
+        rT(0, 0)
+        oC(0, 1, "S")
+        xT(3, 0)
+        sig(0, 0, 0)
+        mm(0, 1, 1)
+        xS(3, 0)
+        cast(2, 0, "S")
+        rT(0, 1)
+        xq(1)
+        oT(1, 2)
+        sig(0, 1, 1)
+        oT(1, 3)
+        gate(0, 0)
+        cast(2, 1, "S")
+        mm(1, 0, 1)
+        gate(0, 1)
+        mm(1, 1, 0)
+        oC(1, 3, "S")
+        rT(1, 0)
         sig(1, 1, 0)
         xT(2, 1)
-        xS(2, 0)
-        oC(1, 1, "S")
-        oT(0, 3)
-        rT(0, 1)
-        oC(0, 3, "S")
-        xS(2, 1)
-        mm(1, 1, 1)
-        mm(0, 1, 1)
-        xq(3)
-        sig(1, 1, 1)
-        oT(1, 3)
-        sig(0, 1, 1)
-        rT(0, 0)
-        oC(0, 0, "S")
-        gate(0, 1)
-        mm(0, 0, 1)
-        oC(1, 3, "S")
-        mm(1, 0, 0)
-        sig(0, 0, 1)
-        xq(2)
-        oT(1, 2)
-        sig(1, 0, 0)
-        gate(0, 0)
-        rT(1, 0)
-        oC(1, 2, "S")
-        rT(1, 1)
-        oq(1, 1)
-        mm(1, 0, 1)
-        yq(0)
-        oT(0, 1)
         sig(1, 0, 1)
-        oq(1, 0)
-        rT(2, 0)
+        oT(1, 1)
+        xS(2, 1)
+        oC(1, 2, "S")
+        xT(2, 0)
+        oC(1, 1, "S")
+        mm(1, 0, 0)
+        yq(0)
+        oT(0, 2)
+        sig(1, 0, 0)
+        xS(2, 0)
+        oT(0, 3)
+        oC(0, 2, "S")
+        mm(1, 1, 1)
         gate(1, 0)
-        mm(2, 0, 1)
-        out_(0, 0, 1)
-        sig(2, 0, 1)
-        gate(1, 1)
-        out_(0, 1, 1)
-        oC(0, 1, "S")
-        mm(2, 1, 1)
+        oC(0, 3, "S")
+        oT(1, 0)
+        sig(1, 1, 1)
+        xq(2)
+        oT(0, 0)
+        oC(1, 0, "S")
+        xT(3, 1)
+        oC(0, 0, "S")
+        oq(1, 1)
+        rT(1, 1)
         oq(0, 1)
-        rT(2, 1)
-        sig(2, 1, 1)
-        oq(0, 0)
-        mm(3, 0, 1)
-        yq(1)
-        mm(2, 1, 0)
-        sig(3, 0, 1)
-        bias(0, 0, 1)
-        out_(0, 0, 0)
-        sig(2, 1, 0)
+        mm(2, 0, 1)
+        gate(1, 1)
         mm(2, 0, 0)
-        biasC(0, 1, 1)
-        gate(2, 1)
-        out_(1, 1, 1)
+        sig(2, 0, 1)
+        rT(3, 0)
         sig(2, 0, 0)
-        biasP(0, 1, 1)
+        xS(3, 1)
+        mm(2, 1, 1)
+        mm(2, 1, 0)
+        sig(2, 1, 1)
+        yq(1)
+        rT(2, 0)
+        sig(2, 1, 0)
+        xq(3)
+        rT(2, 1)
+        oq(1, 0)
         mm(3, 0, 0)
+        oq(0, 0)
+        out_(0, 1, 1)
+        sig(3, 0, 0)
+        gate(2, 1)
+        out_(0, 0, 1)
+        biasC(0, 1, 1)
+        out_(1, 0, 0)
+        biasC(0, 0, 1)
+        biasP(0, 1, 1)
+        out_(0, 1, 0)
+        bias(1, 0, 0)
+        out_(0, 0, 0)
+        bias(0, 1, 0)
+        biasP(0, 0, 1)
+        out_(1, 1, 0)
         biasC(0, 0, 0)
         gate(2, 0)
-        out_(1, 1, 0)
-        sig(3, 0, 0)
-        mm(3, 1, 0)
-        biasP(0, 0, 0)
-        biasC(1, 1, 0)
-        rT(3, 0)
-        bias(1, 1, 1)
-        sig(3, 1, 0)
-        yq(2)
-        out_(0, 1, 0)
-        st(0, 0)
-        gate(3, 0)
-        biasP(1, 1, 0)
-        mm(3, 1, 1)
-        out_(2, 0, 0)
-        sig(3, 1, 1)
-        bias(0, 1, 0)
-        out_(2, 0, 1)
-        st(1, 1)
-        biasC(2, 0, 0)
-        yq1(3, 0)
-        rT(3, 1)
         st(0, 1)
-        bias(2, 0, 1)
-        biasP(2, 0, 0)
-        out_(2, 1, 0)
-        gate(3, 1)
+        out_(1, 1, 1)
+        biasP(0, 0, 0)
+        mm(3, 0, 1)
+        biasC(1, 1, 1)
+        bias(1, 1, 0)
         out_(1, 0, 1)
-        biasC(2, 1, 0)
-        st(2, 0)
-        out_(1, 0, 0)
-        bias(1, 0, 1)
-        biasP(2, 1, 0)
+        sig(3, 0, 1)
+        mm(3, 1, 0)
+        yq(2)
+        st(0, 0)
+        biasC(1, 0, 1)
+        mm(3, 1, 1)
+        gate(3, 0)
+        biasP(1, 1, 1)
+        sig(3, 1, 0)
         out_(2, 1, 1)
-        bias(1, 0, 0)
+        sig(3, 1, 1)
+        out_(2, 0, 1)
+        biasP(1, 0, 1)
+        st(1, 1)
+        biasC(2, 1, 1)
+        out_(2, 1, 0)
+        bias(2, 0, 1)
+        rT(3, 1)
+        bias(2, 1, 0)
+        biasP(2, 1, 1)
         st(1, 0)
-        yq1(3, 1)
-        bias(2, 1, 1)
-        out_(3, 0, 1)
-        out_(3, 0, 0)
+        out_(2, 0, 0)
+        gate(3, 1)
         st(2, 1)
-        bias(3, 0, 1)
-        out_(3, 1, 1)
+        yq1(3, 0)
+        yq1(3, 1)
+        bias(2, 0, 0)
+        out_(3, 0, 0)
+        out_(3, 0, 1)
+        st(2, 0)
         bias(3, 0, 0)
-        st1(3, 0, 1)
         out_(3, 1, 0)
-        bias(3, 1, 1)
+        bias(3, 0, 1)
         st1(3, 0, 0)
+        out_(3, 1, 1)
         bias(3, 1, 0)
-        st1(3, 1, 1)
+        st1(3, 0, 1)
+        bias(3, 1, 1)
         st1(3, 1, 0)
+        st1(3, 1, 1)

@@ -13,458 +13,286 @@ MULT = mybir.AluOpType.mult
 ADD = mybir.AluOpType.add
 SIGMOID = mybir.ActivationFunctionType.Sigmoid
 
-S = 1024
-D = 1024
-FLOPS = 2 * 2 * S * D * D
 P = 128
-NQ = 4
-TQ = S // NQ
-J = TQ // P
+TOKENS = 1024
+D = 1024
+FLOPS = 2 * 2 * TOKENS * D * D
+BLOCKS = 4
+TB = TOKENS // BLOCKS
+J = TB // P
+HALF = 512
+
+ORDER = (
+    "C0 C2 W1 X01 X00 W0 w0 x0 X20 W2 W3 X21 C1 W5 w1 W4 C3 w2 M000 "
+    "X10 X11 x1 W6 W7 M001 M010 X30 X31 O03 O02 M101 R00 w3 R01 O01 G00 O00 "
+    "M011 x2 M100 R10 o0 O10 O12 R11 M110 M111 G01 G10 M211 M210 "
+    "R31 O11 O13 Y0 R21 G11 x3 Y1 o1 R20 G21 P000 M200 P100 M201 P111 G20 "
+    "P110 M310 P010 P101 Y2 S10 M311 P011 M300 M301 S11 G31 S01 P001 y31 P201 S00 "
+    "R30 P210 G30 P200 y30 P211 P310 S20 P311 P300 S21 s310 s311 P301 s300 s301"
+)
+
+WIDENED_BY_VECTOR = ((0, 0), (2, 1))
+BIASED_BY_GPSIMD = ((0, 0, 0), (0, 1, 1), (1, 0, 0), (1, 1, 0), (2, 0, 1), (2, 1, 0))
+WARM_UP = 5
 
 
 def tile_aft_full_pb_kernel(tc, x_bytes, x_scale, wq_w, wq_b, r_aft, out_w, out_b, out):
     nc = tc.nc
-    xb_v = x_bytes[0, :, :].rearrange("(q p j) k -> q p j k", q=NQ, p=P)
-    r_v = r_aft[0, :, :].rearrange("(q p j) k -> q p j k", q=NQ, p=P)
-    out_v = out[0, :, :].rearrange("(q p j) n -> q p j n", q=NQ, p=P)
-    wq_v = wq_w.rearrange("(g m t) k -> g m t k", g=2, m=P)
-    ow_v = out_w.rearrange("(c s m) k -> c m s k", c=2, m=P)
+    x_hbm = x_bytes[0, :, :].rearrange("(b p j) k -> b p j k", b=BLOCKS, p=P)
+    r_hbm = r_aft[0, :, :].rearrange("(b p j) k -> b p j k", b=BLOCKS, p=P)
+    out_hbm = out[0, :, :].rearrange("(b p j) n -> b p j n", b=BLOCKS, p=P)
+    wq_hbm = wq_w.rearrange("(f m t) k -> f m t k", f=2, m=P)
+    ow_hbm = out_w.rearrange("(c s m) k -> c m s k", c=2, m=P)
 
     with ExitStack() as ctx:
         keep = ctx.enter_context(tc.tile_pool(name="keep", bufs=1))
-        pools = {k: ctx.enter_context(tc.psum_pool(name="p" + k, bufs=b)) for k, b in (('q', 2), ('w', 3), ('x', 3))}
+        token_banks = ctx.enter_context(tc.psum_pool(name="token_banks", bufs=3))
+        row_banks = ctx.enter_context(tc.psum_pool(name="row_banks", bufs=2))
+        query_banks = ctx.enter_context(tc.psum_pool(name="query_banks", bufs=3))
         ctx.enter_context(tc.manual_schedule())
 
-        sc = keep.tile([P, 2, 4], F32)
-        wqb = keep.tile([P, 2, 4], BF16)
-        outb = keep.tile([P, D], BF16)
-        ident = keep.tile([P, P], F32)
-        warm = keep.tile([P, 1], F32)
-        zz = keep.tile([P, 512], BF16)
-        x_raw = keep.tile([P, NQ, J, D], U8, align_bytes=64)
-        x_bf = keep.tile([P, NQ, J, D], BF16, align_bytes=64)
+        x_mult = keep.tile([P, 2, 4], F32)
+        query_bias = keep.tile([P, 2, 4], BF16)
+        out_bias = keep.tile([P, D], BF16)
+        identity = keep.tile([P, P], F32)
+        zeros = keep.tile([P, HALF], BF16)
+        one_column = keep.tile([P, 1], F32)
+        x_raw = keep.tile([P, BLOCKS, J, D], U8, align_bytes=64)
+        x_wide = keep.tile([P, BLOCKS, J, D], BF16, align_bytes=64)
+        r_raw = keep.tile([P, BLOCKS, J, D], BF16, align_bytes=64)
         wq_raw = keep.tile([P, 8, D], BF16, align_bytes=64)
         ow_raw = keep.tile([P, 2, 4, D], BF16, align_bytes=64)
-        r_raw = keep.tile([P, NQ, J, D], BF16, align_bytes=64)
-        xg = keep.tile([P, NQ, 2, TQ * 4], BF16, align_bytes=64)
-        x_codes = keep.tile([P, NQ, 2, TQ], U32, align_bytes=64)
-        x_scales = keep.tile([P, NQ, 2, TQ], U8, align_bytes=64)
-        wg = keep.tile([P, 8, 2, P * 4], BF16, align_bytes=64)
-        w_codes = keep.tile([P, 8, 2, P], U32, align_bytes=64)
-        w_scales = keep.tile([P, 8, 2, P], U8, align_bytes=64)
-        og = keep.tile([P, 2, 2, 4, P * 4], BF16, align_bytes=64)
-        o_codes = keep.tile([P, 2, 2, 512], U32, align_bytes=64)
-        o_scales = keep.tile([P, 2, 2, 512], U8, align_bytes=64)
-        sg = keep.tile([P, 2, 2, 4, TQ], F32, align_bytes=64)
-        yg = keep.tile([P, NQ, 2, TQ * 4], BF16, align_bytes=64)
-        y_codes = keep.tile([P, NQ, 2, TQ], U32, align_bytes=64)
-        y_scales = keep.tile([P, NQ, 2, TQ], U8, align_bytes=64)
-        res = keep.tile([P, NQ, J, D], F32, align_bytes=64)
+        x_kin = keep.tile([P, BLOCKS, 2, TB * 4], BF16, align_bytes=64)
+        x_codes = keep.tile([P, BLOCKS, 2, TB], U32, align_bytes=64)
+        x_scales = keep.tile([P, BLOCKS, 2, TB], U8, align_bytes=64)
+        wq_kin = keep.tile([P, 8, 2, P * 4], BF16, align_bytes=64)
+        wq_codes = keep.tile([P, 8, 2, P], U32, align_bytes=64)
+        wq_scales = keep.tile([P, 8, 2, P], U8, align_bytes=64)
+        ow_kin = keep.tile([P, 2, 2, 4, P * 4], BF16, align_bytes=64)
+        ow_codes = keep.tile([P, 2, 2, HALF], U32, align_bytes=64)
+        ow_scales = keep.tile([P, 2, 2, HALF], U8, align_bytes=64)
+        gate_sig = keep.tile([P, 2, 2, 4, TB], F32, align_bytes=64)
+        y_kin = keep.tile([P, BLOCKS, 2, TB * 4], BF16, align_bytes=64)
+        y_codes = keep.tile([P, BLOCKS, 2, TB], U32, align_bytes=64)
+        y_scales = keep.tile([P, BLOCKS, 2, TB], U8, align_bytes=64)
+        result = keep.tile([P, BLOCKS, J, D], F32, align_bytes=64)
+
+        x_words = x_wide[:].bitcast(F32)
+        r_words = r_raw[:].bitcast(F32)
+        wq_words = wq_raw[:].bitcast(F32)
+        ow_words = ow_raw[:].bitcast(F32)
+        wq_kin_words = wq_kin[:].bitcast(F32)
+        ow_kin_words = ow_kin[:].bitcast(F32)
         bank = {}
 
-        x_words = x_bf[:].bitcast(F32)
-        r_words = r_raw[:].bitcast(F32)
-        w_words = wq_raw[:].bitcast(F32)
-        o_words = ow_raw[:].bitcast(F32)
-        wg_words = wg[:].bitcast(F32)
-        og_words = og[:].bitcast(F32)
+        def load_x(b):
+            nc.sync.dma_start(out=x_raw[:, b], in_=x_hbm[b])
 
-        def sc_():
-            nc.scalar.dma_start(out=sc[:], in_=x_scale[0, :, :].rearrange("o (g p t) -> p (o g) t", p=P, t=4))
+        def load_wq(first, count):
+            f, t = first // 4, first % 4
+            nc.sync.dma_start(out=wq_raw[:, first : first + count, :], in_=wq_hbm[f][:, t : t + count, :])
 
-        def bq():
-            nc.scalar.dma_start(out=wqb[:], in_=wq_b.rearrange("(g p t) -> p g t", p=P, t=4))
+        def load_ow(c, s):
+            nc.sync.dma_start(out=ow_raw[:, c, s : s + 2, :], in_=ow_hbm[c][:, s : s + 2, :])
 
-        def id_():
-            make_identity(nc, ident[:])
-            nc.vector.memset(zz[:], 0.0)
-            nc.vector.memset(warm[:], 0.0)
-            nc.scalar.activation(out=warm[:], in_=warm[:], func=SIGMOID)
+        def load_r(b):
+            nc.sync.dma_start(out=r_raw[:, b], in_=r_hbm[b])
 
-        def lx(q):
-            nc.sync.dma_start(out=x_raw[:, q], in_=xb_v[q])
+        def widen(b):
+            for j in range(J):
+                codes = x_raw[:, b, j, :].bitcast(FP8)
+                if (b, j) in WIDENED_BY_VECTOR:
+                    nc.vector.tensor_copy(out=x_wide[:, b, j, :], in_=codes)
+                else:
+                    nc.scalar.copy(out=x_wide[:, b, j, :], in_=codes)
 
-        def l1(s):
-            nc.sync.dma_start(out=wq_raw[:, s, :], in_=wq_v[s // 4][:, s % 4, :])
-
-        def lw(i):
-            g, t = i // 2, 2 * (i % 2)
-            nc.sync.dma_start(out=wq_raw[:, 2 * i : 2 * i + 2, :], in_=wq_v[g][:, t : t + 2, :])
-
-        def lo(i):
-            c, s = i // 2, 2 * (i % 2)
-            nc.sync.dma_start(out=ow_raw[:, c, s : s + 2, :], in_=ow_v[c][:, s : s + 2, :])
-
-        def lr(q):
-            nc.sync.dma_start(out=r_raw[:, q], in_=r_v[q])
-
-        def lb():
-            nc.sync.dma_start(out=outb[:], in_=out_b.partition_broadcast(P))
-
-        def cast(q, j, e):
-            src = x_raw[:, q, j, :].bitcast(FP8)
-            if e == "V":
-                nc.vector.tensor_copy(out=x_bf[:, q, j, :], in_=src)
-            else:
-                nc.scalar.copy(out=x_bf[:, q, j, :], in_=src)
-
-        def copy(e, dst, src):
-            if e == "V":
-                nc.vector.tensor_copy(out=dst, in_=src)
-            else:
-                nc.scalar.copy(out=dst, in_=src)
-
-        def busy(flat, n):
-            for i in range(n):
-                nc.tensor.matmul(flat, lhsT=zz[:, :P], rhs=zz[:], start=True, stop=True)
-
-        def turn_tokens(words, q, g, n):
-            b = pools["x"].tile([P, 2, TQ], F32, name="x")
-            busy(b[:].rearrange("p u c -> p (u c)"), n)
+        def turn_tokens(words, b, g):
+            turned = token_banks.tile([P, 2, TB], F32, name="turned")
             for u in range(2):
                 for j in range(J):
                     nc.tensor.transpose(
-                        b[:, u, j * P : (j + 1) * P],
-                        words[:, q, j, 256 * g + u : 256 * (g + 1) : 2],
-                        ident[:],
+                        turned[:, u, j * P : (j + 1) * P],
+                        words[:, b, j, 256 * g + u : 256 * (g + 1) : 2],
+                        identity[:],
                     )
-            return b
+            return turned
 
-        def turn_rows(row_words, n):
-            b = pools["w"].tile([P, 4, P], F32, name="w")
-            busy(b[:].rearrange("p i m -> p (i m)"), n)
+        def turn_rows(row_words):
+            rows = row_banks.tile([P, 4, P], F32, name="rows")
             for i in range(4):
                 g, u = i // 2, i % 2
-                nc.tensor.transpose(b[:, i, :], row_words[:, 256 * g + u : 256 * (g + 1) : 2], ident[:])
-            return b
+                nc.tensor.transpose(rows[:, i, :], row_words[:, 256 * g + u : 256 * (g + 1) : 2], identity[:])
+            return rows
 
         def by_k(flat):
             return flat.rearrange("p (c u e) -> p c u e", u=2, e=2)
 
-        def bank_by_k(b):
-            return b[:].bitcast(BF16).rearrange("p u (c e) -> p c u e", e=2)
+        def bank_by_k(turned):
+            return turned[:].bitcast(BF16).rearrange("p u (c e) -> p c u e", e=2)
 
-        def xT(q, g, n=0):
-            bank["x", q, g] = turn_tokens(x_words, q, g, n)
+        def turn_x(b, g):
+            turned = turn_tokens(x_words, b, g)
+            scale = x_mult[:, g, :].rearrange("p (u e) -> p u e", u=2).unsqueeze(1).to_broadcast([P, TB, 2, 2])
+            nc.vector.tensor_tensor(out=by_k(x_kin[:, b, g, :]), in0=bank_by_k(turned), in1=scale, op=MULT)
 
-        def xS(q, g):
-            scale = sc[:, g, :].rearrange("p (u e) -> p u e", u=2).unsqueeze(1).to_broadcast([P, TQ, 2, 2])
-            nc.vector.tensor_tensor(out=by_k(xg[:, q, g, :]), in0=bank_by_k(bank["x", q, g]), in1=scale, op=MULT)
-
-        def xq(q):
+        def quantise_x(b):
             nc.vector.quantize_mx(
-                out=x_codes[:, q].rearrange("p g c -> p (g c)").bitcast(FP8X4),
-                scales=x_scales[:, q].rearrange("p g c -> p (g c)"),
-                in_=xg[:, q].rearrange("p g c -> p (g c)"),
+                out=x_codes[:, b].rearrange("p g c -> p (g c)").bitcast(FP8X4),
+                scales=x_scales[:, b].rearrange("p g c -> p (g c)"),
+                in_=x_kin[:, b].rearrange("p g c -> p (g c)"),
             )
 
-        def wT(i, n=0):
-            bank["w", i] = turn_rows(w_words[:, i, :], n)
-
-        def wC(i, e):
-            copy(
-                e,
-                wg_words[:, i].rearrange("p g (m u) -> p g m u", u=2),
-                bank["w", i][:].rearrange("p (g u) m -> p g m u", u=2),
+        def turn_wq(i):
+            rows = turn_rows(wq_words[:, i, :])
+            nc.scalar.copy(
+                out=wq_kin_words[:, i].rearrange("p g (m u) -> p g m u", u=2),
+                in_=rows[:].rearrange("p (g u) m -> p g m u", u=2),
             )
 
-        def wq(i):
+        def quantise_wq(i):
             pair = slice(2 * i, 2 * i + 2)
             nc.vector.quantize_mx(
-                out=w_codes[:, pair].rearrange("p s g m -> p (s g m)").bitcast(FP8X4),
-                scales=w_scales[:, pair].rearrange("p s g m -> p (s g m)"),
-                in_=wg[:, pair].rearrange("p s g m -> p (s g m)"),
+                out=wq_codes[:, pair].rearrange("p s g m -> p (s g m)").bitcast(FP8X4),
+                scales=wq_scales[:, pair].rearrange("p s g m -> p (s g m)"),
+                in_=wq_kin[:, pair].rearrange("p s g m -> p (s g m)"),
             )
 
-        def oT(c, s, n=0):
-            bank["o", c, s] = turn_rows(o_words[:, c, s, :], n)
-
-        def oC(c, s, e):
-            copy(
-                e,
-                og_words[:, c, :, s, :].rearrange("p g (m u) -> p g m u", u=2),
-                bank["o", c, s][:].rearrange("p (g u) m -> p g m u", u=2),
+        def turn_ow(c, s):
+            rows = turn_rows(ow_words[:, c, s, :])
+            nc.scalar.copy(
+                out=ow_kin_words[:, c, :, s, :].rearrange("p g (m u) -> p g m u", u=2),
+                in_=rows[:].rearrange("p (g u) m -> p g m u", u=2),
             )
 
-        def oq(c, g):
-            nc.vector.quantize_mx(
-                out=o_codes[:, c, g, :].bitcast(FP8X4),
-                scales=o_scales[:, c, g, :],
-                in_=og[:, c, g].rearrange("p s m -> p (s m)"),
-            )
+        def quantise_ow(c):
+            for g in range(2):
+                nc.vector.quantize_mx(
+                    out=ow_codes[:, c, g, :].bitcast(FP8X4),
+                    scales=ow_scales[:, c, g, :],
+                    in_=ow_kin[:, c, g].rearrange("p s m -> p (s m)"),
+                )
 
-        def rT(q, f, n=0):
-            bank["r", q, f] = turn_tokens(r_words, q, f, n)
+        def turn_r(b, f):
+            bank["r", b, f] = turn_tokens(r_words, b, f)
 
-        def mm(q, f, h, n=0):
-            b = pools["q"].tile([P, 2, TQ], F32, name="q")
-            bank["q", q, f, h] = b
-            busy(b[:].rearrange("p u c -> p (u c)"), n)
+        def query(b, f, h):
+            q = query_banks.tile([P, 2, TB], F32, name="q")
             for i in range(2):
-                t = 2 * h + i
                 for g in range(2):
                     nc.tensor.matmul_mx(
-                        out=b[:, i, :],
-                        lhsT=w_codes[:, 4 * f + t, g, :].bitcast(FP8X4),
-                        lhsT_scale=w_scales[:, 4 * f + t, g, :],
-                        rhs=x_codes[:, q, g, :].bitcast(FP8X4),
-                        rhs_scale=x_scales[:, q, g, :],
+                        out=q[:, i, :],
+                        lhsT=wq_codes[:, 4 * f + 2 * h + i, g, :].bitcast(FP8X4),
+                        lhsT_scale=wq_scales[:, 4 * f + 2 * h + i, g, :],
+                        rhs=x_codes[:, b, g, :].bitcast(FP8X4),
+                        rhs_scale=x_scales[:, b, g, :],
                         start=(g == 0),
                         stop=(g == 1),
                     )
-
-        def sig(q, f, h):
             for i in range(2):
                 t = 2 * h + i
                 nc.scalar.activation(
-                    out=sg[:, q % 2, f, t, :], in_=bank["q", q, f, h][:, i, :], func=SIGMOID, bias=wqb[:, f, t : t + 1]
+                    out=gate_sig[:, b % 2, f, t, :], in_=q[:, i, :], func=SIGMOID, bias=query_bias[:, f, t : t + 1]
                 )
 
-        def gate(q, f):
+        def gate(b, f):
             nc.vector.tensor_tensor(
-                out=by_k(yg[:, q, f, :]),
-                in0=bank_by_k(bank["r", q, f]),
-                in1=sg[:, q % 2, f].rearrange("p (u e) c -> p c u e", u=2),
+                out=by_k(y_kin[:, b, f, :]),
+                in0=bank_by_k(bank["r", b, f]),
+                in1=gate_sig[:, b % 2, f].rearrange("p (u e) c -> p c u e", u=2),
                 op=MULT,
             )
 
-        def yq(q):
+        def quantise_y(b):
             nc.vector.quantize_mx(
-                out=y_codes[:, q].rearrange("p g c -> p (g c)").bitcast(FP8X4),
-                scales=y_scales[:, q].rearrange("p g c -> p (g c)"),
-                in_=yg[:, q].rearrange("p g c -> p (g c)"),
+                out=y_codes[:, b].rearrange("p f c -> p (f c)").bitcast(FP8X4),
+                scales=y_scales[:, b].rearrange("p f c -> p (f c)"),
+                in_=y_kin[:, b].rearrange("p f c -> p (f c)"),
             )
 
-        def yq1(q, f):
+        def quantise_y_half(b, f):
             nc.vector.quantize_mx(
-                out=y_codes[:, q, f, :].bitcast(FP8X4),
-                scales=y_scales[:, q, f, :],
-                in_=yg[:, q, f, :],
+                out=y_codes[:, b, f, :].bitcast(FP8X4), scales=y_scales[:, b, f, :], in_=y_kin[:, b, f, :]
             )
 
-        def out_(q, j, c, n=0):
-            b = pools["w"].tile([P, 512], F32, name="w")
-            bank["out", q, j, c] = b
-            busy(b[:], n)
+        def project(b, j, c):
+            rows = row_banks.tile([P, HALF], F32, name="rows")
             for g in range(2):
                 nc.tensor.matmul_mx(
-                    out=b[:],
-                    lhsT=y_codes[:, q, g, j * P : (j + 1) * P].bitcast(FP8X4),
-                    lhsT_scale=y_scales[:, q, g, j * P : (j + 1) * P],
-                    rhs=o_codes[:, c, g, :].bitcast(FP8X4),
-                    rhs_scale=o_scales[:, c, g, :],
+                    out=rows[:],
+                    lhsT=y_codes[:, b, g, j * P : (j + 1) * P].bitcast(FP8X4),
+                    lhsT_scale=y_scales[:, b, g, j * P : (j + 1) * P],
+                    rhs=ow_codes[:, c, g, :].bitcast(FP8X4),
+                    rhs_scale=ow_scales[:, c, g, :],
                     start=(g == 0),
                     stop=(g == 1),
                 )
+            if (b, j, c) in BIASED_BY_GPSIMD:
+                columns = slice(HALF * c, HALF * (c + 1))
+                nc.scalar.copy(out=result[:, b, j, columns], in_=rows[:])
+                for first in (HALF * c, HALF * c + HALF // 2):
+                    part = slice(first, first + HALF // 2)
+                    nc.gpsimd.tensor_tensor(
+                        out=result[:, b, j, part], in0=result[:, b, j, part], in1=out_bias[:, part], op=ADD
+                    )
+            else:
+                columns = slice(HALF * c, HALF * (c + 1))
+                nc.vector.tensor_tensor(
+                    out=result[:, b, j, columns], in0=rows[:], in1=out_bias[:, columns], op=ADD
+                )
 
-        def bias(q, j, c):
-            cols = slice(512 * c, 512 * (c + 1))
-            nc.vector.tensor_tensor(
-                out=res[:, q, j, cols], in0=bank["out", q, j, c][:], in1=outb[:, cols], op=ADD
-            )
+        def store(b, j):
+            nc.sync.dma_start(out=out_hbm[b][:, j, :], in_=result[:, b, j, :])
 
-        def biasC(q, j, c):
-            cols = slice(512 * c, 512 * (c + 1))
-            nc.scalar.copy(out=res[:, q, j, cols], in_=bank["out", q, j, c][:])
+        def store_half(b, j, c):
+            columns = slice(HALF * c, HALF * (c + 1))
+            nc.sync.dma_start(out=out_hbm[b][:, j, columns], in_=result[:, b, j, columns])
 
-        def biasP(q, j, c):
-            cols = slice(512 * c, 512 * (c + 1))
-            nc.gpsimd.tensor_tensor(out=res[:, q, j, cols], in0=res[:, q, j, cols], in1=outb[:, cols], op=ADD)
+        nc.scalar.dma_start(out=x_mult[:], in_=x_scale[0, :, :].rearrange("o (g p t) -> p (o g) t", p=P, t=4))
+        nc.scalar.dma_start(out=query_bias[:], in_=wq_b.rearrange("(f p t) -> p f t", p=P, t=4))
+        make_identity(nc, identity[:])
+        nc.vector.memset(zeros[:], 0.0)
+        nc.vector.memset(one_column[:], 0.0)
+        nc.scalar.activation(out=one_column[:], in_=one_column[:], func=SIGMOID)
 
-        def st(q, j):
-            nc.sync.dma_start(out=out_v[q][:, j, :], in_=res[:, q, j, :])
+        load_x(0)
+        load_wq(1, 1)
+        load_x(2)
+        load_wq(0, 1)
+        load_wq(2, 2)
+        load_x(1)
+        load_wq(4, 2)
+        load_x(3)
+        load_wq(6, 2)
+        load_ow(0, 2)
+        load_ow(1, 0)
+        load_ow(0, 0)
+        load_r(0)
+        load_r(1)
+        load_ow(1, 2)
+        load_r(3)
+        load_r(2)
+        nc.sync.dma_start(out=out_bias[:], in_=out_b.partition_broadcast(P))
 
-        def st1(q, j, c):
-            cols = slice(512 * c, 512 * (c + 1))
-            nc.sync.dma_start(out=out_v[q][:, j, cols], in_=res[:, q, j, cols])
+        warm = query_banks.tile([P, HALF], F32, name="q")
+        for i in range(WARM_UP):
+            nc.tensor.matmul(warm[:], lhsT=zeros[:, :P], rhs=zeros[:], start=True, stop=True)
 
-        bq()
-        id_()
-        lx(0)
-        sc_()
-        lw(2)
-        lw(1)
-        l1(1)
-        lw(3)
-        l1(0)
-        lx(1)
-        lx(2)
-        lo(0)
-        cast(0, 1, "S")
-        lx(3)
-        cast(0, 0, "S")
-        wT(5, n=8)
-        wT(4)
-        wC(5, "V")
-        lr(3)
-        xT(0, 1)
-        wC(4, "S")
-        lr(0)
-        wT(3)
-        xS(0, 1)
-        wT(2)
-        lr(2)
-        wq(2)
-        xT(0, 0)
-        wC(2, "S")
-        lo(3)
-        wC(3, "V")
-        wT(7)
-        lr(1)
-        xS(0, 0)
-        wT(6)
-        lo(2)
-        wC(7, "S")
-        wT(0)
-        cast(1, 1, "S")
-        wq(1)
-        lo(1)
-        wT(1)
-        xq(0)
-        wC(6, "S")
-        lb()
-        wC(1, "V")
-        mm(0, 0, 1)
-        cast(1, 0, "S")
-        wq(3)
-        mm(0, 1, 0)
-        cast(3, 0, "V")
-        wC(0, "S")
-        xT(1, 0)
-        sig(0, 0, 1)
-        wq(0)
-        xT(1, 1)
-        sig(0, 1, 0)
-        xS(1, 0)
-        oT(0, 1)
-        cast(3, 1, "S")
-        mm(0, 0, 0)
-        xS(1, 1)
-        rT(0, 0)
-        oC(0, 1, "S")
-        xT(3, 0)
-        sig(0, 0, 0)
-        mm(0, 1, 1)
-        xS(3, 0)
-        cast(2, 0, "S")
-        rT(0, 1)
-        xq(1)
-        oT(1, 2)
-        sig(0, 1, 1)
-        oT(1, 3)
-        gate(0, 0)
-        cast(2, 1, "S")
-        mm(1, 0, 1)
-        gate(0, 1)
-        mm(1, 1, 0)
-        oC(1, 3, "S")
-        rT(1, 0)
-        sig(1, 1, 0)
-        xT(2, 1)
-        sig(1, 0, 1)
-        oT(1, 1)
-        xS(2, 1)
-        oC(1, 2, "S")
-        xT(2, 0)
-        oC(1, 1, "S")
-        mm(1, 0, 0)
-        yq(0)
-        oT(0, 2)
-        sig(1, 0, 0)
-        xS(2, 0)
-        oT(0, 3)
-        oC(0, 2, "S")
-        mm(1, 1, 1)
-        gate(1, 0)
-        oC(0, 3, "S")
-        oT(1, 0)
-        sig(1, 1, 1)
-        xq(2)
-        oT(0, 0)
-        oC(1, 0, "S")
-        xT(3, 1)
-        oC(0, 0, "S")
-        oq(1, 1)
-        rT(1, 1)
-        oq(0, 1)
-        mm(2, 0, 1)
-        gate(1, 1)
-        mm(2, 0, 0)
-        sig(2, 0, 1)
-        rT(3, 0)
-        sig(2, 0, 0)
-        xS(3, 1)
-        mm(2, 1, 1)
-        mm(2, 1, 0)
-        sig(2, 1, 1)
-        yq(1)
-        rT(2, 0)
-        sig(2, 1, 0)
-        xq(3)
-        rT(2, 1)
-        oq(1, 0)
-        mm(3, 0, 0)
-        oq(0, 0)
-        out_(0, 1, 1)
-        sig(3, 0, 0)
-        gate(2, 1)
-        out_(0, 0, 1)
-        biasC(0, 1, 1)
-        out_(1, 0, 0)
-        biasC(0, 0, 1)
-        biasP(0, 1, 1)
-        out_(0, 1, 0)
-        bias(1, 0, 0)
-        out_(0, 0, 0)
-        bias(0, 1, 0)
-        biasP(0, 0, 1)
-        out_(1, 1, 0)
-        biasC(0, 0, 0)
-        gate(2, 0)
-        st(0, 1)
-        out_(1, 1, 1)
-        biasP(0, 0, 0)
-        mm(3, 0, 1)
-        biasC(1, 1, 1)
-        bias(1, 1, 0)
-        out_(1, 0, 1)
-        sig(3, 0, 1)
-        mm(3, 1, 0)
-        yq(2)
-        st(0, 0)
-        biasC(1, 0, 1)
-        mm(3, 1, 1)
-        gate(3, 0)
-        biasP(1, 1, 1)
-        sig(3, 1, 0)
-        out_(2, 1, 1)
-        sig(3, 1, 1)
-        out_(2, 0, 1)
-        biasP(1, 0, 1)
-        st(1, 1)
-        biasC(2, 1, 1)
-        out_(2, 1, 0)
-        bias(2, 0, 1)
-        rT(3, 1)
-        bias(2, 1, 0)
-        biasP(2, 1, 1)
-        st(1, 0)
-        out_(2, 0, 0)
-        gate(3, 1)
-        st(2, 1)
-        yq1(3, 0)
-        yq1(3, 1)
-        bias(2, 0, 0)
-        out_(3, 0, 0)
-        out_(3, 0, 1)
-        st(2, 0)
-        bias(3, 0, 0)
-        out_(3, 1, 0)
-        bias(3, 0, 1)
-        st1(3, 0, 0)
-        out_(3, 1, 1)
-        bias(3, 1, 0)
-        st1(3, 0, 1)
-        bias(3, 1, 1)
-        st1(3, 1, 0)
-        st1(3, 1, 1)
+        steps = {
+            "C": widen,
+            "X": turn_x,
+            "x": quantise_x,
+            "W": turn_wq,
+            "w": quantise_wq,
+            "O": turn_ow,
+            "o": quantise_ow,
+            "R": turn_r,
+            "M": query,
+            "G": gate,
+            "Y": quantise_y,
+            "y": quantise_y_half,
+            "P": project,
+            "S": store,
+            "s": store_half,
+        }
+        for step in ORDER.split():
+            steps[step[0]](*[int(digit) for digit in step[1:]])

from contextlib import ExitStack

import concourse.mybir as mybir
from concourse.masks import make_identity

F32 = mybir.dt.float32
BF16 = mybir.dt.bfloat16
U32 = mybir.dt.uint32
U8 = mybir.dt.uint8
FP8 = mybir.dt.float8_e4m3fn
FP8X4 = mybir.dt.float8_e4m3fn_x4
MULT = mybir.AluOpType.mult
ADD = mybir.AluOpType.add
SIGMOID = mybir.ActivationFunctionType.Sigmoid

P = 128
TOKENS = 1024
D = 1024
FLOPS = 2 * 2 * TOKENS * D * D
BLOCKS = 4
TB = TOKENS // BLOCKS
J = TB // P
HALF = 512

ORDER = (
    "C0 C2 W1 X01 X00 W0 w0 x0 X20 W2 W3 X21 C1 W5 w1 W4 C3 w2 M000 "
    "X10 X11 x1 W6 W7 M001 M010 X30 X31 O03 O02 M101 R00 w3 R01 O01 G00 O00 "
    "M011 x2 M100 R10 o0 O10 O12 R11 M110 M111 G01 G10 M211 M210 "
    "R31 O11 O13 Y0 R21 G11 x3 Y1 o1 R20 G21 P000 M200 P100 M201 P111 G20 "
    "P110 M310 P010 P101 Y2 S10 M311 P011 M300 M301 S11 G31 S01 P001 y31 P201 S00 "
    "R30 P210 G30 P200 y30 P211 P310 S20 P311 P300 S21 s310 s311 P301 s300 s301"
)

WIDENED_BY_VECTOR = ((0, 0), (2, 1))
BIASED_BY_GPSIMD = ((0, 0, 0), (0, 1, 1), (1, 0, 0), (1, 1, 0), (2, 0, 1), (2, 1, 0))
WARM_UP = 5


def tile_aft_full_pb_kernel(tc, x_bytes, x_scale, wq_w, wq_b, r_aft, out_w, out_b, out):
    nc = tc.nc
    x_hbm = x_bytes[0, :, :].rearrange("(b p j) k -> b p j k", b=BLOCKS, p=P)
    r_hbm = r_aft[0, :, :].rearrange("(b p j) k -> b p j k", b=BLOCKS, p=P)
    out_hbm = out[0, :, :].rearrange("(b p j) n -> b p j n", b=BLOCKS, p=P)
    wq_hbm = wq_w.rearrange("(f m t) k -> f m t k", f=2, m=P)
    ow_hbm = out_w.rearrange("(c s m) k -> c m s k", c=2, m=P)

    with ExitStack() as ctx:
        keep = ctx.enter_context(tc.tile_pool(name="keep", bufs=1))
        token_banks = ctx.enter_context(tc.psum_pool(name="token_banks", bufs=3))
        row_banks = ctx.enter_context(tc.psum_pool(name="row_banks", bufs=2))
        query_banks = ctx.enter_context(tc.psum_pool(name="query_banks", bufs=3))
        ctx.enter_context(tc.manual_schedule())

        x_mult = keep.tile([P, 2, 4], F32)
        query_bias = keep.tile([P, 2, 4], BF16)
        out_bias = keep.tile([P, D], BF16)
        identity = keep.tile([P, P], F32)
        zeros = keep.tile([P, HALF], BF16)
        one_column = keep.tile([P, 1], F32)
        x_raw = keep.tile([P, BLOCKS, J, D], U8, align_bytes=64)
        x_wide = keep.tile([P, BLOCKS, J, D], BF16, align_bytes=64)
        r_raw = keep.tile([P, BLOCKS, J, D], BF16, align_bytes=64)
        wq_raw = keep.tile([P, 8, D], BF16, align_bytes=64)
        ow_raw = keep.tile([P, 2, 4, D], BF16, align_bytes=64)
        x_kin = keep.tile([P, BLOCKS, 2, TB * 4], BF16, align_bytes=64)
        x_codes = keep.tile([P, BLOCKS, 2, TB], U32, align_bytes=64)
        x_scales = keep.tile([P, BLOCKS, 2, TB], U8, align_bytes=64)
        wq_kin = keep.tile([P, 8, 2, P * 4], BF16, align_bytes=64)
        wq_codes = keep.tile([P, 8, 2, P], U32, align_bytes=64)
        wq_scales = keep.tile([P, 8, 2, P], U8, align_bytes=64)
        ow_kin = keep.tile([P, 2, 2, 4, P * 4], BF16, align_bytes=64)
        ow_codes = keep.tile([P, 2, 2, HALF], U32, align_bytes=64)
        ow_scales = keep.tile([P, 2, 2, HALF], U8, align_bytes=64)
        gate_sig = keep.tile([P, 2, 2, 4, TB], F32, align_bytes=64)
        y_kin = keep.tile([P, BLOCKS, 2, TB * 4], BF16, align_bytes=64)
        y_codes = keep.tile([P, BLOCKS, 2, TB], U32, align_bytes=64)
        y_scales = keep.tile([P, BLOCKS, 2, TB], U8, align_bytes=64)
        result = keep.tile([P, BLOCKS, J, D], F32, align_bytes=64)

        x_words = x_wide[:].bitcast(F32)
        r_words = r_raw[:].bitcast(F32)
        wq_words = wq_raw[:].bitcast(F32)
        ow_words = ow_raw[:].bitcast(F32)
        wq_kin_words = wq_kin[:].bitcast(F32)
        ow_kin_words = ow_kin[:].bitcast(F32)
        bank = {}

        def load_x(b):
            nc.sync.dma_start(out=x_raw[:, b], in_=x_hbm[b])

        def load_wq(first, count):
            f, t = first // 4, first % 4
            nc.sync.dma_start(out=wq_raw[:, first : first + count, :], in_=wq_hbm[f][:, t : t + count, :])

        def load_ow(c, s):
            nc.sync.dma_start(out=ow_raw[:, c, s : s + 2, :], in_=ow_hbm[c][:, s : s + 2, :])

        def load_r(b):
            nc.sync.dma_start(out=r_raw[:, b], in_=r_hbm[b])

        def widen(b):
            for j in range(J):
                codes = x_raw[:, b, j, :].bitcast(FP8)
                if (b, j) in WIDENED_BY_VECTOR:
                    nc.vector.tensor_copy(out=x_wide[:, b, j, :], in_=codes)
                else:
                    nc.scalar.copy(out=x_wide[:, b, j, :], in_=codes)

        def turn_tokens(words, b, g):
            turned = token_banks.tile([P, 2, TB], F32, name="turned")
            for u in range(2):
                for j in range(J):
                    nc.tensor.transpose(
                        turned[:, u, j * P : (j + 1) * P],
                        words[:, b, j, 256 * g + u : 256 * (g + 1) : 2],
                        identity[:],
                    )
            return turned

        def turn_rows(row_words):
            rows = row_banks.tile([P, 4, P], F32, name="rows")
            for i in range(4):
                g, u = i // 2, i % 2
                nc.tensor.transpose(rows[:, i, :], row_words[:, 256 * g + u : 256 * (g + 1) : 2], identity[:])
            return rows

        def by_k(flat):
            return flat.rearrange("p (c u e) -> p c u e", u=2, e=2)

        def bank_by_k(turned):
            return turned[:].bitcast(BF16).rearrange("p u (c e) -> p c u e", e=2)

        def turn_x(b, g):
            turned = turn_tokens(x_words, b, g)
            scale = x_mult[:, g, :].rearrange("p (u e) -> p u e", u=2).unsqueeze(1).to_broadcast([P, TB, 2, 2])
            nc.vector.tensor_tensor(out=by_k(x_kin[:, b, g, :]), in0=bank_by_k(turned), in1=scale, op=MULT)

        def quantise_x(b):
            nc.vector.quantize_mx(
                out=x_codes[:, b].rearrange("p g c -> p (g c)").bitcast(FP8X4),
                scales=x_scales[:, b].rearrange("p g c -> p (g c)"),
                in_=x_kin[:, b].rearrange("p g c -> p (g c)"),
            )

        def turn_wq(i):
            rows = turn_rows(wq_words[:, i, :])
            nc.scalar.copy(
                out=wq_kin_words[:, i].rearrange("p g (m u) -> p g m u", u=2),
                in_=rows[:].rearrange("p (g u) m -> p g m u", u=2),
            )

        def quantise_wq(i):
            pair = slice(2 * i, 2 * i + 2)
            nc.vector.quantize_mx(
                out=wq_codes[:, pair].rearrange("p s g m -> p (s g m)").bitcast(FP8X4),
                scales=wq_scales[:, pair].rearrange("p s g m -> p (s g m)"),
                in_=wq_kin[:, pair].rearrange("p s g m -> p (s g m)"),
            )

        def turn_ow(c, s):
            rows = turn_rows(ow_words[:, c, s, :])
            nc.scalar.copy(
                out=ow_kin_words[:, c, :, s, :].rearrange("p g (m u) -> p g m u", u=2),
                in_=rows[:].rearrange("p (g u) m -> p g m u", u=2),
            )

        def quantise_ow(c):
            for g in range(2):
                nc.vector.quantize_mx(
                    out=ow_codes[:, c, g, :].bitcast(FP8X4),
                    scales=ow_scales[:, c, g, :],
                    in_=ow_kin[:, c, g].rearrange("p s m -> p (s m)"),
                )

        def turn_r(b, f):
            bank["r", b, f] = turn_tokens(r_words, b, f)

        def query(b, f, h):
            q = query_banks.tile([P, 2, TB], F32, name="q")
            for i in range(2):
                for g in range(2):
                    nc.tensor.matmul_mx(
                        out=q[:, i, :],
                        lhsT=wq_codes[:, 4 * f + 2 * h + i, g, :].bitcast(FP8X4),
                        lhsT_scale=wq_scales[:, 4 * f + 2 * h + i, g, :],
                        rhs=x_codes[:, b, g, :].bitcast(FP8X4),
                        rhs_scale=x_scales[:, b, g, :],
                        start=(g == 0),
                        stop=(g == 1),
                    )
            for i in range(2):
                t = 2 * h + i
                nc.scalar.activation(
                    out=gate_sig[:, b % 2, f, t, :], in_=q[:, i, :], func=SIGMOID, bias=query_bias[:, f, t : t + 1]
                )

        def gate(b, f):
            nc.vector.tensor_tensor(
                out=by_k(y_kin[:, b, f, :]),
                in0=bank_by_k(bank["r", b, f]),
                in1=gate_sig[:, b % 2, f].rearrange("p (u e) c -> p c u e", u=2),
                op=MULT,
            )

        def quantise_y(b):
            nc.vector.quantize_mx(
                out=y_codes[:, b].rearrange("p f c -> p (f c)").bitcast(FP8X4),
                scales=y_scales[:, b].rearrange("p f c -> p (f c)"),
                in_=y_kin[:, b].rearrange("p f c -> p (f c)"),
            )

        def quantise_y_half(b, f):
            nc.vector.quantize_mx(
                out=y_codes[:, b, f, :].bitcast(FP8X4), scales=y_scales[:, b, f, :], in_=y_kin[:, b, f, :]
            )

        def project(b, j, c):
            rows = row_banks.tile([P, HALF], F32, name="rows")
            for g in range(2):
                nc.tensor.matmul_mx(
                    out=rows[:],
                    lhsT=y_codes[:, b, g, j * P : (j + 1) * P].bitcast(FP8X4),
                    lhsT_scale=y_scales[:, b, g, j * P : (j + 1) * P],
                    rhs=ow_codes[:, c, g, :].bitcast(FP8X4),
                    rhs_scale=ow_scales[:, c, g, :],
                    start=(g == 0),
                    stop=(g == 1),
                )
            if (b, j, c) in BIASED_BY_GPSIMD:
                columns = slice(HALF * c, HALF * (c + 1))
                nc.scalar.copy(out=result[:, b, j, columns], in_=rows[:])
                for first in (HALF * c, HALF * c + HALF // 2):
                    part = slice(first, first + HALF // 2)
                    nc.gpsimd.tensor_tensor(
                        out=result[:, b, j, part], in0=result[:, b, j, part], in1=out_bias[:, part], op=ADD
                    )
            else:
                columns = slice(HALF * c, HALF * (c + 1))
                nc.vector.tensor_tensor(
                    out=result[:, b, j, columns], in0=rows[:], in1=out_bias[:, columns], op=ADD
                )

        def store(b, j):
            nc.sync.dma_start(out=out_hbm[b][:, j, :], in_=result[:, b, j, :])

        def store_half(b, j, c):
            columns = slice(HALF * c, HALF * (c + 1))
            nc.sync.dma_start(out=out_hbm[b][:, j, columns], in_=result[:, b, j, columns])

        nc.scalar.dma_start(out=x_mult[:], in_=x_scale[0, :, :].rearrange("o (g p t) -> p (o g) t", p=P, t=4))
        nc.scalar.dma_start(out=query_bias[:], in_=wq_b.rearrange("(f p t) -> p f t", p=P, t=4))
        make_identity(nc, identity[:])
        nc.vector.memset(zeros[:], 0.0)
        nc.vector.memset(one_column[:], 0.0)
        nc.scalar.activation(out=one_column[:], in_=one_column[:], func=SIGMOID)

        load_x(0)
        load_wq(1, 1)
        load_x(2)
        load_wq(0, 1)
        load_wq(2, 2)
        load_x(1)
        load_wq(4, 2)
        load_x(3)
        load_wq(6, 2)
        load_ow(0, 2)
        load_ow(1, 0)
        load_ow(0, 0)
        load_r(0)
        load_r(1)
        load_ow(1, 2)
        load_r(3)
        load_r(2)
        nc.sync.dma_start(out=out_bias[:], in_=out_b.partition_broadcast(P))

        warm = query_banks.tile([P, HALF], F32, name="q")
        for i in range(WARM_UP):
            nc.tensor.matmul(warm[:], lhsT=zeros[:, :P], rhs=zeros[:], start=True, stop=True)

        steps = {
            "C": widen,
            "X": turn_x,
            "x": quantise_x,
            "W": turn_wq,
            "w": quantise_wq,
            "O": turn_ow,
            "o": quantise_ow,
            "R": turn_r,
            "M": query,
            "G": gate,
            "Y": quantise_y,
            "y": quantise_y_half,
            "P": project,
            "S": store,
            "s": store_half,
        }
        for step in ORDER.split():
            steps[step[0]](*[int(digit) for digit in step[1:]])
